import numpy as np
import ml_dtypes


def mxq(x, axis, fmt="e4m3"):
    dtype, down = {"e4m3": (ml_dtypes.float8_e4m3fn, 7), "e5m2": (ml_dtypes.float8_e5m2, 14)}[fmt]
    v = np.moveaxis(np.asarray(x, np.float32).astype(ml_dtypes.bfloat16).astype(np.float64), axis, -1)
    blocks = v.reshape(v.shape[:-1] + (-1, 32))
    amax = np.abs(blocks).max(-1, keepdims=True)
    byte = np.maximum(np.where(amax > 0, np.frexp(amax)[1] - 1 + 127, 0) - down, 1)
    scale = np.exp2(byte - 127.0)
    codes = (blocks / scale).astype(np.float32).astype(dtype).astype(np.float64)
    return np.moveaxis((codes * scale).reshape(v.shape), -1, axis)


WIDE = False


def mx_kscale(k):
    if not WIDE:
        return np.ones(k)
    levels = np.array([10, -10, 5, -5, 0])
    if k % 512:
        return np.exp2(np.random.permutation(np.resize(levels, k // 32))).repeat(32)
    a = np.empty((k // 512, 16))
    for p in range(k // 512):
        a[p, :8] = np.random.permutation(np.resize(levels, 8))
        for g in range(8):
            far = levels[np.abs(levels - a[p, g]) >= 10]
            a[p, g + 8] = far[np.random.randint(len(far))]
    return np.exp2(a.ravel()).repeat(32)


BF16 = ml_dtypes.bfloat16


def bf(x):
    return np.asarray(x, np.float32).astype(BF16)


def f64(x):
    return np.asarray(x).astype(np.float64)


B, Q, S, D = 16, 256, 512, 512
K = D + D


def sigmoid(v):
    return 1.0 / (1.0 + np.exp(-v))


def setup_inputs():
    t = mx_kscale(D)
    s = np.concatenate([np.ones(D), t])
    return {"query": bf(np.random.standard_normal((B, Q, D)) * 0.25),
            "weighted_ctx": bf(np.random.standard_normal((B, Q, D)) * 0.12 * t),
            "W_lin": bf(np.random.standard_normal((K, D)) * 5.0 / np.sqrt(K) / s[:, None]),
            "b_lin": bf(np.random.standard_normal(D) * 0.3),
            "W_gate": bf(np.random.standard_normal((K, D)) * 5.0 / np.sqrt(K) / s[:, None]),
            "b_gate": bf(np.random.standard_normal(D) * 0.3)}


def reference(query, weighted_ctx, W_lin, b_lin, W_gate, b_gate):
    q = f64(query)
    cat = mxq(np.concatenate([q, f64(weighted_ctx)], axis=2), 2, "e4m3")
    h = np.tanh((cat @ mxq(f64(W_lin), 0, "e4m3")) + f64(b_lin))
    g = sigmoid((cat @ mxq(f64(W_gate), 0, "e4m3")) + f64(b_gate))
    return q * g + h * (1.0 - g)

@@ -1,0 +1,262 @@
+from contextlib import ExitStack
+
+import concourse.mybir as mybir
+from concourse.masks import make_identity
+
+F32 = mybir.dt.float32
+BF16 = mybir.dt.bfloat16
+U32 = mybir.dt.uint32
+U8 = mybir.dt.uint8
+FP8X4 = mybir.dt.float8_e4m3fn_x4
+ACT = mybir.ActivationFunctionType
+ALU = mybir.AluOpType
+
+P = 128
+PACK = 4
+K_PASS = P * PACK
+TOKENS = 4096
+D = 512
+PASSES = 2
+GROUP = 512
+TILES = GROUP // P
+GROUPS = TOKENS // GROUP
+HALVES = 2
+UNITS = GROUPS * HALVES
+LEAD = 2
+VECTOR_TOKENS = 320
+
+FLOPS = 2 * TOKENS * (PASSES * K_PASS) * (2 * D)
+
+
+def tile_smcmr_pb_t_kernel(tc, query, weighted_ctx, W_lin, b_lin, W_gate, b_gate, out):
+    nc = tc.nc
+    with ExitStack() as ctx:
+        ctx.enter_context(tc.manual_schedule())
+        const = ctx.enter_context(tc.tile_pool(name="const", bufs=1))
+        inputs = ctx.enter_context(tc.tile_pool(name="inputs", bufs=1))
+        weights = ctx.enter_context(tc.tile_pool(name="weights", bufs=1))
+        stage = ctx.enter_context(tc.tile_pool(name="stage", bufs=3))
+        acts = ctx.enter_context(tc.tile_pool(name="acts", bufs=2))
+        deltas = ctx.enter_context(tc.tile_pool(name="deltas", bufs=4))
+        results = ctx.enter_context(tc.tile_pool(name="results", bufs=2))
+        psum_in = ctx.enter_context(tc.psum_pool(name="psum_in", bufs=2))
+        psum_acc = ctx.enter_context(tc.psum_pool(name="psum_acc", bufs=4))
+        psum_out = ctx.enter_context(tc.psum_pool(name="psum_out", bufs=2))
+
+        by_group = "(G p i) f -> G p (i f)"
+        q_rows = query.flatten_outer_dims().rearrange(by_group, p=P, i=TILES)
+        c_rows = weighted_ctx.flatten_outer_dims().rearrange(by_group, p=P, i=TILES)
+        out_rows = out.flatten_outer_dims().rearrange(by_group, p=P, i=TILES)
+
+        ident = const.tile([P, P], F32)
+        make_identity(nc, ident[:])
+        bias_raw = const.tile([P, 2 * 64], BF16)
+        zero = const.tile([P, 1], F32)
+        nc.vector.memset(zero[:], 0.0)
+        warm = const.tile([P, 1], F32)
+        nc.scalar.activation(out=warm[:], in_=zero[:], func=ACT.Sigmoid)
+
+        q_sb = {}
+        c_sb = {}
+
+        def load_group(G):
+            q_sb[G] = inputs.tile([P, TILES * D], BF16, name="q%d" % G)
+            nc.sync.dma_start(out=q_sb[G][:], in_=q_rows[G])
+            c_sb[G] = inputs.tile([P, TILES * D], BF16, name="c%d" % G)
+            nc.sync.dma_start(out=c_sb[G][:], in_=c_rows[G])
+
+        def load_weight(W, name):
+            raw = weights.tile([P, PASSES * PACK * D], BF16, name=name)
+            nc.sync.dma_start(
+                out=raw[:].rearrange("p (g r) -> p g r", g=PASSES),
+                in_=W.rearrange("(g p t) n -> p g (t n)", g=PASSES, t=PACK),
+            )
+            return raw
+
+        load_group(0)
+        nc.sync.dma_start(out=bias_raw[:, 0:PACK], in_=b_lin.rearrange("(p t) -> p t", t=PACK))
+        nc.sync.dma_start(out=bias_raw[:, 64 : 64 + PACK], in_=b_gate.rearrange("(p t) -> p t", t=PACK))
+        raw_lin = load_weight(W_lin, "raw_lin")
+        raw_gate = load_weight(W_gate, "raw_gate")
+        for G in range(1, GROUPS):
+            load_group(G)
+
+        bias_lin = const.tile([P, PACK], F32)
+        bias_gate_neg = const.tile([P, PACK], F32)
+
+        def spread_biases():
+            nc.vector.tensor_copy(out=bias_lin[:], in_=bias_raw[:, 0:PACK])
+            nc.vector.tensor_scalar_mul(out=bias_gate_neg[:], in0=bias_raw[:, 64 : 64 + PACK], scalar1=-1.0)
+
+        W_COLS = HALVES * PASSES * 2 * P
+        grouped_w = {}
+        codes_w = {}
+        scales_w = {}
+        for name in ("gate", "lin"):
+            grouped_w[name] = weights.tile([P, W_COLS * PACK], BF16, name="grouped_" + name, align_bytes=64)
+            codes_w[name] = weights.tile([P, W_COLS], U32, name="codes_" + name, align_bytes=64)
+            scales_w[name] = weights.tile([P, W_COLS], U8, name="scales_" + name, align_bytes=64)
+
+        def regroup_weight(copy, raw, name, half):
+            rows = raw[:].rearrange("p (g t n) -> p g t n", g=PASSES, t=PACK)
+            words = grouped_w[name][:].rearrange(
+                "p (u g e j t) -> p u g e j t", u=HALVES, g=PASSES, e=2, t=PACK
+            )
+            for g in range(PASSES):
+                copy(
+                    out=words[:, half, g],
+                    in_=rows[:, g].rearrange("p t (j h e) -> p h e j t", h=HALVES, e=2)[:, half],
+                )
+
+        def quantise_weight(name, half):
+            cols = slice(half * PASSES * 2 * P, (half + 1) * PASSES * 2 * P)
+            nc.vector.quantize_mx(
+                out=codes_w[name][:, cols].bitcast(FP8X4),
+                scales=scales_w[name][:, cols],
+                in_=grouped_w[name][:, half * PASSES * 2 * P * PACK : (half + 1) * PASSES * 2 * P * PACK],
+            )
+
+        grouped = {}
+        codes = {}
+        scales = {}
+        keep = {}
+        cand = {}
+        delta = {}
+        banks_out = {}
+        result = {}
+
+        def transpose_in(v):
+            G, g = divmod(v, PASSES)
+            if g == 0:
+                grouped[G] = stage.tile([P, PASSES * GROUP * PACK], BF16, name="grouped", align_bytes=64)
+            words = (q_sb[G] if g == 0 else c_sb[G])[:].bitcast(F32)
+            pairs = grouped[G][:].bitcast(F32).rearrange("p (g c u) -> p g c u", g=PASSES, u=2)
+            for b in range(2):
+                xt = psum_in.tile([P, 2, 2 * P], F32, tag="xt")
+                for u in range(2):
+                    for ii in range(2):
+                        first = (2 * b + ii) * 2 * P
+                        nc.tensor.transpose(
+                            out=xt[:, u, ii * P : (ii + 1) * P],
+                            in_=words[:, first + u : first + 2 * P : 2],
+                            identity=ident[:],
+                        )
+                nc.scalar.copy(
+                    out=pairs[:, g, b * 2 * P : (b + 1) * 2 * P, :], in_=xt[:].rearrange("p u c -> p c u")
+                )
+
+        def quantise_in(v):
+            G, g = divmod(v, PASSES)
+            if g == 0:
+                codes[G] = stage.tile([P, PASSES * GROUP], U32, name="codes", align_bytes=64)
+                scales[G] = stage.tile([P, PASSES * GROUP], U8, name="scales", align_bytes=64)
+            nc.vector.quantize_mx(
+                out=codes[G][:, g * GROUP : (g + 1) * GROUP].bitcast(FP8X4),
+                scales=scales[G][:, g * GROUP : (g + 1) * GROUP],
+                in_=grouped[G][:, g * GROUP * PACK : (g + 1) * GROUP * PACK],
+            )
+
+        def product(name, G, half, e):
+            acc = psum_acc.tile([P, GROUP], F32)
+            for g in range(PASSES):
+                first = ((half * PASSES + g) * 2 + e) * P
+                nc.tensor.matmul_mx(
+                    out=acc[:],
+                    lhsT=codes_w[name][:, first : first + P].bitcast(FP8X4),
+                    lhsT_scale=scales_w[name][:, first : first + P],
+                    rhs=codes[G][:, g * GROUP : (g + 1) * GROUP].bitcast(FP8X4),
+                    rhs_scale=scales[G][:, g * GROUP : (g + 1) * GROUP],
+                    start=(g == 0),
+                    stop=(g == PASSES - 1),
+                )
+            return acc
+
+        def gates(s):
+            G, half = divmod(s, HALVES)
+            keep[s] = acts.tile([P, 2, GROUP], F32, name="keep")
+            cand[s] = acts.tile([P, 2, GROUP], F32, name="cand")
+            for e in range(2):
+                t = 2 * half + e
+                acc = product("lin", G, half, e)
+                nc.scalar.activation(
+                    out=cand[s][:, e, :], in_=acc[:], func=ACT.Tanh, bias=bias_lin[:, t : t + 1], scale=1.0
+                )
+            for e in range(2):
+                t = 2 * half + e
+                acc = product("gate", G, half, e)
+                nc.scalar.activation(
+                    out=keep[s][:, e, :], in_=acc[:], func=ACT.Sigmoid, bias=bias_gate_neg[:, t : t + 1], scale=-1.0
+                )
+
+        def difference(s):
+            G, half = divmod(s, HALVES)
+            q_t = grouped[G][:].rearrange("p (g c t) -> p g c t", g=PASSES, t=PACK)
+            delta[s] = deltas.tile([P, 2, GROUP], F32, name="delta")
+            for engine, tokens in ((nc.gpsimd, slice(VECTOR_TOKENS, GROUP)), (nc.vector, slice(0, VECTOR_TOKENS))):
+                engine.tensor_tensor(
+                    out=delta[s][:, :, tokens],
+                    in0=q_t[:, 0, tokens, 2 * half : 2 * half + 2].rearrange("p c e -> p e c"),
+                    in1=cand[s][:, :, tokens],
+                    op=ALU.subtract,
+                )
+
+        def weigh(s):
+            nc.vector.tensor_tensor(out=delta[s][:], in0=keep[s][:], in1=delta[s][:], op=ALU.mult)
+
+        def transpose_out(r):
+            G, b = divmod(r, HALVES)
+            banks_out[r] = []
+            for ii in range(2):
+                first = (2 * b + ii) * P
+                ot = psum_out.tile([P, PACK, P], F32)
+                for t in range(PACK):
+                    nc.tensor.transpose(
+                        out=ot[:, t, :], in_=delta[2 * G + t // 2][:, t % 2, first : first + P], identity=ident[:]
+                    )
+                banks_out[r].append(ot)
+
+        def finish(r):
+            G, b = divmod(r, HALVES)
+            if b == 0:
+                result[G] = results.tile([P, TILES * D], F32, name="result")
+            o_view = result[G][:].rearrange("p (i j t) -> p i j t", i=TILES, t=PACK)
+            q_view = q_sb[G][:].rearrange("p (i j t) -> p i j t", i=TILES, t=PACK)
+            for ii in range(2):
+                nc.vector.tensor_tensor(
+                    out=o_view[:, 2 * b + ii],
+                    in0=q_view[:, 2 * b + ii],
+                    in1=banks_out[r][ii][:].rearrange("p t j -> p j t"),
+                    op=ALU.subtract,
+                )
+            rows = slice(2 * b * D, (2 * b + 2) * D)
+            nc.sync.dma_start(out=out_rows[G][:, rows], in_=result[G][:, rows])
+
+        transpose_in(0)
+        quantise_in(0)
+        transpose_in(1)
+        regroup_weight(nc.vector.tensor_copy, raw_lin, "lin", 0)
+        quantise_in(1)
+        spread_biases()
+        quantise_weight("lin", 0)
+        regroup_weight(nc.scalar.copy, raw_lin, "lin", 1)
+        regroup_weight(nc.vector.tensor_copy, raw_gate, "gate", 0)
+        quantise_weight("gate", 0)
+        quantise_weight("lin", 1)
+        regroup_weight(nc.vector.tensor_copy, raw_gate, "gate", 1)
+        quantise_weight("gate", 1)
+
+        for k in range(UNITS + 4):
+            if k + LEAD < UNITS:
+                transpose_in(k + LEAD)
+            if k < UNITS:
+                gates(k)
+            if 0 <= k - 3 < UNITS:
+                transpose_out(k - 3)
+            if 0 <= k - 4:
+                finish(k - 4)
+            if 0 <= k - 1 < UNITS:
+                difference(k - 1)
+            if k + LEAD < UNITS:
+                quantise_in(k + LEAD)
+            if 0 <= k - 1 < UNITS:
+                weigh(k - 1)

@@ -17,13 +17,9 @@ K_PASS = P * PACK
 TOKENS = 4096
 D = 512
 PASSES = 2
-GROUP = 512
-TILES = GROUP // P
-GROUPS = TOKENS // GROUP
 HALVES = 2
-UNITS = GROUPS * HALVES
-LEAD = 2
-VECTOR_TOKENS = 320
+BLOCKS = [256, 512, 512, 512, 512, 512, 512, 512, 256]
+UNITS = len(BLOCKS) * HALVES
 
 FLOPS = 2 * TOKENS * (PASSES * K_PASS) * (2 * D)
 
@@ -43,10 +39,11 @@ def tile_smcmr_pb_t_kernel(tc, query, weighted_ctx, W_lin, b_lin, W_gate, b_gate
         psum_acc = ctx.enter_context(tc.psum_pool(name="psum_acc", bufs=4))
         psum_out = ctx.enter_context(tc.psum_pool(name="psum_out", bufs=2))
 
-        by_group = "(G p i) f -> G p (i f)"
-        q_rows = query.flatten_outer_dims().rearrange(by_group, p=P, i=TILES)
-        c_rows = weighted_ctx.flatten_outer_dims().rearrange(by_group, p=P, i=TILES)
-        out_rows = out.flatten_outer_dims().rearrange(by_group, p=P, i=TILES)
+        starts = [sum(BLOCKS[:B]) for B in range(len(BLOCKS))]
+
+        def rows(array, B):
+            block = array.flatten_outer_dims()[starts[B] : starts[B] + BLOCKS[B], :]
+            return block.rearrange("(p i) f -> p (i f)", p=P)
 
         ident = const.tile([P, P], F32)
         make_identity(nc, ident[:])
@@ -59,30 +56,31 @@ def tile_smcmr_pb_t_kernel(tc, query, weighted_ctx, W_lin, b_lin, W_gate, b_gate
         q_sb = {}
         c_sb = {}
 
-        def load_group(G):
-            q_sb[G] = inputs.tile([P, TILES * D], BF16, name="q%d" % G)
-            nc.sync.dma_start(out=q_sb[G][:], in_=q_rows[G])
-            c_sb[G] = inputs.tile([P, TILES * D], BF16, name="c%d" % G)
-            nc.sync.dma_start(out=c_sb[G][:], in_=c_rows[G])
+        def load_operand(B, g):
+            kept, array, name = ((q_sb, query, "q"), (c_sb, weighted_ctx, "c"))[g]
+            kept[B] = inputs.tile([P, BLOCKS[B] // P * D], BF16, name="%s%d" % (name, B))
+            nc.sync.dma_start(out=kept[B][:], in_=rows(array, B))
 
-        def load_weight(W, name):
-            raw = weights.tile([P, PASSES * PACK * D], BF16, name=name)
-            nc.sync.dma_start(
-                out=raw[:].rearrange("p (g r) -> p g r", g=PASSES),
-                in_=W.rearrange("(g p t) n -> p g (t n)", g=PASSES, t=PACK),
-            )
-            return raw
+        def load_block(B):
+            for g in range(PASSES):
+                load_operand(B, g)
 
-        load_group(0)
-        nc.sync.dma_start(out=bias_raw[:, 0:PACK], in_=b_lin.rearrange("(p t) -> p t", t=PACK))
-        nc.sync.dma_start(out=bias_raw[:, 64 : 64 + PACK], in_=b_gate.rearrange("(p t) -> p t", t=PACK))
-        raw_lin = load_weight(W_lin, "raw_lin")
-        raw_gate = load_weight(W_gate, "raw_gate")
-        for G in range(1, GROUPS):
-            load_group(G)
+        raw_w = {}
+
+        def load_weight(name, passes=range(PASSES)):
+            W = {"lin": W_lin, "gate": W_gate}[name]
+            if name not in raw_w:
+                raw_w[name] = weights.tile([P, PASSES * PACK * D], BF16, name="raw_" + name)
+            rows_w = W.rearrange("(g p t) n -> g p (t n)", g=PASSES, t=PACK)
+            for g in passes:
+                nc.sync.dma_start(out=raw_w[name][:, g * PACK * D : (g + 1) * PACK * D], in_=rows_w[g])
 
         bias_lin = const.tile([P, PACK], F32)
         bias_gate_neg = const.tile([P, PACK], F32)
+
+        def load_biases():
+            nc.sync.dma_start(out=bias_raw[:, 0:PACK], in_=b_lin.rearrange("(p t) -> p t", t=PACK))
+            nc.sync.dma_start(out=bias_raw[:, 64 : 64 + PACK], in_=b_gate.rearrange("(p t) -> p t", t=PACK))
 
         def spread_biases():
             nc.vector.tensor_copy(out=bias_lin[:], in_=bias_raw[:, 0:PACK])
@@ -97,15 +95,15 @@ def tile_smcmr_pb_t_kernel(tc, query, weighted_ctx, W_lin, b_lin, W_gate, b_gate
             codes_w[name] = weights.tile([P, W_COLS], U32, name="codes_" + name, align_bytes=64)
             scales_w[name] = weights.tile([P, W_COLS], U8, name="scales_" + name, align_bytes=64)
 
-        def regroup_weight(copy, raw, name, half):
-            rows = raw[:].rearrange("p (g t n) -> p g t n", g=PASSES, t=PACK)
+        def regroup_weight(copy, name, half, passes=range(PASSES)):
+            raw = raw_w[name][:].rearrange("p (g t n) -> p g t n", g=PASSES, t=PACK)
             words = grouped_w[name][:].rearrange(
                 "p (u g e j t) -> p u g e j t", u=HALVES, g=PASSES, e=2, t=PACK
             )
-            for g in range(PASSES):
+            for g in passes:
                 copy(
                     out=words[:, half, g],
-                    in_=rows[:, g].rearrange("p t (j h e) -> p h e j t", h=HALVES, e=2)[:, half],
+                    in_=raw[:, g].rearrange("p t (j h e) -> p h e j t", h=HALVES, e=2)[:, half],
                 )
 
         def quantise_weight(name, half):
@@ -126,73 +124,83 @@ def tile_smcmr_pb_t_kernel(tc, query, weighted_ctx, W_lin, b_lin, W_gate, b_gate
         result = {}
 
         def transpose_in(v):
-            G, g = divmod(v, PASSES)
+            B, g = divmod(v, PASSES)
+            n = BLOCKS[B]
             if g == 0:
-                grouped[G] = stage.tile([P, PASSES * GROUP * PACK], BF16, name="grouped", align_bytes=64)
-            words = (q_sb[G] if g == 0 else c_sb[G])[:].bitcast(F32)
-            pairs = grouped[G][:].bitcast(F32).rearrange("p (g c u) -> p g c u", g=PASSES, u=2)
-            for b in range(2):
-                xt = psum_in.tile([P, 2, 2 * P], F32, tag="xt")
+                grouped[B] = stage.tile([P, PASSES * n * PACK], BF16, name="grouped", align_bytes=64)
+            words = (q_sb[B] if g == 0 else c_sb[B])[:].bitcast(F32)
+            pairs = grouped[B][:].bitcast(F32).rearrange("p (g c u) -> p g c u", g=PASSES, u=2)
+            width = min(n, 2 * P)
+            for b in range(n // width):
+                xt = psum_in.tile([P, 2, width], F32, tag="xt")
                 for u in range(2):
-                    for ii in range(2):
+                    for ii in range(width // P):
                         first = (2 * b + ii) * 2 * P
-                        nc.tensor.transpose(
-                            out=xt[:, u, ii * P : (ii + 1) * P],
-                            in_=words[:, first + u : first + 2 * P : 2],
-                            identity=ident[:],
-                        )
+                        in_words = words[:, first + u : first + 2 * P : 2]
+                        nc.tensor.transpose(out=xt[:, u, ii * P : (ii + 1) * P], in_=in_words, identity=ident[:])
                 nc.scalar.copy(
-                    out=pairs[:, g, b * 2 * P : (b + 1) * 2 * P, :], in_=xt[:].rearrange("p u c -> p c u")
+                    out=pairs[:, g, b * width : (b + 1) * width, :], in_=xt[:].rearrange("p u c -> p c u")
                 )
 
         def quantise_in(v):
-            G, g = divmod(v, PASSES)
+            B, g = divmod(v, PASSES)
+            n = BLOCKS[B]
             if g == 0:
-                codes[G] = stage.tile([P, PASSES * GROUP], U32, name="codes", align_bytes=64)
-                scales[G] = stage.tile([P, PASSES * GROUP], U8, name="scales", align_bytes=64)
+                codes[B] = stage.tile([P, PASSES * n], U32, name="codes", align_bytes=64)
+                scales[B] = stage.tile([P, PASSES * n], U8, name="scales", align_bytes=64)
             nc.vector.quantize_mx(
-                out=codes[G][:, g * GROUP : (g + 1) * GROUP].bitcast(FP8X4),
-                scales=scales[G][:, g * GROUP : (g + 1) * GROUP],
-                in_=grouped[G][:, g * GROUP * PACK : (g + 1) * GROUP * PACK],
+                out=codes[B][:, g * n : (g + 1) * n].bitcast(FP8X4),
+                scales=scales[B][:, g * n : (g + 1) * n],
+                in_=grouped[B][:, g * n * PACK : (g + 1) * n * PACK],
             )
 
-        def product(name, G, half, e):
-            acc = psum_acc.tile([P, GROUP], F32)
+        def product(name, B, half, e):
+            n = BLOCKS[B]
+            acc = psum_acc.tile([P, n], F32, tag="acc")
             for g in range(PASSES):
                 first = ((half * PASSES + g) * 2 + e) * P
                 nc.tensor.matmul_mx(
                     out=acc[:],
                     lhsT=codes_w[name][:, first : first + P].bitcast(FP8X4),
                     lhsT_scale=scales_w[name][:, first : first + P],
-                    rhs=codes[G][:, g * GROUP : (g + 1) * GROUP].bitcast(FP8X4),
-                    rhs_scale=scales[G][:, g * GROUP : (g + 1) * GROUP],
+                    rhs=codes[B][:, g * n : (g + 1) * n].bitcast(FP8X4),
+                    rhs_scale=scales[B][:, g * n : (g + 1) * n],
                     start=(g == 0),
                     stop=(g == PASSES - 1),
                 )
             return acc
 
-        def gates(s):
-            G, half = divmod(s, HALVES)
-            keep[s] = acts.tile([P, 2, GROUP], F32, name="keep")
-            cand[s] = acts.tile([P, 2, GROUP], F32, name="cand")
+        def candidates(s):
+            B, half = divmod(s, HALVES)
+            n = BLOCKS[B]
+            cand[s] = acts.tile([P, 2, n], F32, name="cand")
             for e in range(2):
                 t = 2 * half + e
-                acc = product("lin", G, half, e)
+                acc = product("lin", B, half, e)
                 nc.scalar.activation(
                     out=cand[s][:, e, :], in_=acc[:], func=ACT.Tanh, bias=bias_lin[:, t : t + 1], scale=1.0
                 )
+
+        def gates(s):
+            B, half = divmod(s, HALVES)
+            n = BLOCKS[B]
+            keep[s] = acts.tile([P, 2, n], F32, name="keep")
             for e in range(2):
                 t = 2 * half + e
-                acc = product("gate", G, half, e)
+                acc = product("gate", B, half, e)
                 nc.scalar.activation(
                     out=keep[s][:, e, :], in_=acc[:], func=ACT.Sigmoid, bias=bias_gate_neg[:, t : t + 1], scale=-1.0
                 )
 
         def difference(s):
-            G, half = divmod(s, HALVES)
-            q_t = grouped[G][:].rearrange("p (g c t) -> p g c t", g=PASSES, t=PACK)
-            delta[s] = deltas.tile([P, 2, GROUP], F32, name="delta")
-            for engine, tokens in ((nc.gpsimd, slice(VECTOR_TOKENS, GROUP)), (nc.vector, slice(0, VECTOR_TOKENS))):
+            B, half = divmod(s, HALVES)
+            n = BLOCKS[B]
+            q_t = grouped[B][:].rearrange("p (g c t) -> p g c t", g=PASSES, t=PACK)
+            delta[s] = deltas.tile([P, 2, n], F32, name="delta")
+            share = n * (5 if B < len(BLOCKS) - 1 else 0) // 8
+            for engine, tokens in ((nc.gpsimd, slice(share, n)), (nc.vector, slice(0, share))):
+                if tokens.start == tokens.stop:
+                    continue
                 engine.tensor_tensor(
                     out=delta[s][:, :, tokens],
                     in0=q_t[:, 0, tokens, 2 * half : 2 * half + 2].rearrange("p c e -> p e c"),
@@ -204,59 +212,194 @@ def tile_smcmr_pb_t_kernel(tc, query, weighted_ctx, W_lin, b_lin, W_gate, b_gate
             nc.vector.tensor_tensor(out=delta[s][:], in0=keep[s][:], in1=delta[s][:], op=ALU.mult)
 
         def transpose_out(r):
-            G, b = divmod(r, HALVES)
+            B, b = r
             banks_out[r] = []
-            for ii in range(2):
+            for ii in range(min(BLOCKS[B] // P, 2)):
                 first = (2 * b + ii) * P
-                ot = psum_out.tile([P, PACK, P], F32)
+                ot = psum_out.tile([P, PACK, P], F32, tag="ot")
                 for t in range(PACK):
                     nc.tensor.transpose(
-                        out=ot[:, t, :], in_=delta[2 * G + t // 2][:, t % 2, first : first + P], identity=ident[:]
+                        out=ot[:, t, :], in_=delta[2 * B + t // 2][:, t % 2, first : first + P], identity=ident[:]
                     )
                 banks_out[r].append(ot)
 
         def finish(r):
-            G, b = divmod(r, HALVES)
+            B, b = r
+            tiles = BLOCKS[B] // P
             if b == 0:
-                result[G] = results.tile([P, TILES * D], F32, name="result")
-            o_view = result[G][:].rearrange("p (i j t) -> p i j t", i=TILES, t=PACK)
-            q_view = q_sb[G][:].rearrange("p (i j t) -> p i j t", i=TILES, t=PACK)
-            for ii in range(2):
+                result[B] = results.tile([P, tiles * D], F32, name="result")
+            o_view = result[B][:].rearrange("p (i j t) -> p i j t", i=tiles, t=PACK)
+            q_view = q_sb[B][:].rearrange("p (i j t) -> p i j t", i=tiles, t=PACK)
+            for ii in range(min(tiles, 2)):
+                turned = banks_out[r][ii][:].rearrange("p t j -> p j t")
                 nc.vector.tensor_tensor(
-                    out=o_view[:, 2 * b + ii],
-                    in0=q_view[:, 2 * b + ii],
-                    in1=banks_out[r][ii][:].rearrange("p t j -> p j t"),
-                    op=ALU.subtract,
+                    out=o_view[:, 2 * b + ii], in0=q_view[:, 2 * b + ii], in1=turned, op=ALU.subtract
                 )
-            rows = slice(2 * b * D, (2 * b + 2) * D)
-            nc.sync.dma_start(out=out_rows[G][:, rows], in_=result[G][:, rows])
+            cols = slice(2 * b * D, (2 * b + min(tiles, 2)) * D)
+            nc.sync.dma_start(out=rows(out, B)[:, cols], in_=result[B][:, cols])
 
+        load_operand(0, 0)
+        load_weight("lin", [0])
+        load_operand(0, 1)
+        load_weight("lin", [1])
+        load_biases()
+        load_weight("gate", [0])
+        load_weight("gate", [1])
+        load_operand(1, 0)
+        load_operand(1, 1)
+        for B in range(2, len(BLOCKS)):
+            load_block(B)
+        V, S = nc.vector.tensor_copy, nc.scalar.copy
         transpose_in(0)
+        regroup_weight(V, "lin", 0, [0])
+        regroup_weight(V, "lin", 1, [0])
         quantise_in(0)
+        regroup_weight(V, "lin", 0, [1])
+        regroup_weight(S, "lin", 1, [1])
         transpose_in(1)
-        regroup_weight(nc.vector.tensor_copy, raw_lin, "lin", 0)
-        quantise_in(1)
         spread_biases()
         quantise_weight("lin", 0)
-        regroup_weight(nc.scalar.copy, raw_lin, "lin", 1)
-        regroup_weight(nc.vector.tensor_copy, raw_gate, "gate", 0)
-        quantise_weight("gate", 0)
+        quantise_in(1)
         quantise_weight("lin", 1)
-        regroup_weight(nc.vector.tensor_copy, raw_gate, "gate", 1)
+        regroup_weight(S, "gate", 1, [0])
+        candidates(0)
+        candidates(1)
+        regroup_weight(V, "gate", 0, [0])
+        regroup_weight(V, "gate", 0, [1])
+        quantise_weight("gate", 0)
+        transpose_in(2)
+        regroup_weight(V, "gate", 1, [1])
         quantise_weight("gate", 1)
-
-        for k in range(UNITS + 4):
-            if k + LEAD < UNITS:
-                transpose_in(k + LEAD)
-            if k < UNITS:
-                gates(k)
-            if 0 <= k - 3 < UNITS:
-                transpose_out(k - 3)
-            if 0 <= k - 4:
-                finish(k - 4)
-            if 0 <= k - 1 < UNITS:
-                difference(k - 1)
-            if k + LEAD < UNITS:
-                quantise_in(k + LEAD)
-            if 0 <= k - 1 < UNITS:
-                weigh(k - 1)
+        gates(0)
+        transpose_in(3)
+        quantise_in(2)
+        gates(1)
+        difference(0)
+        quantise_in(3)
+        weigh(0)
+        transpose_in(4)
+        candidates(2)
+        gates(2)
+        difference(1)
+        quantise_in(4)
+        weigh(1)
+        transpose_in(5)
+        candidates(3)
+        gates(3)
+        transpose_out((0,0))
+        difference(2)
+        quantise_in(5)
+        weigh(2)
+        transpose_in(6)
+        candidates(4)
+        gates(4)
+        finish((0,0))
+        difference(3)
+        quantise_in(6)
+        weigh(3)
+        transpose_in(7)
+        candidates(5)
+        gates(5)
+        transpose_out((1,0))
+        difference(4)
+        quantise_in(7)
+        weigh(4)
+        transpose_in(8)
+        candidates(6)
+        gates(6)
+        transpose_out((1,1))
+        finish((1,0))
+        difference(5)
+        quantise_in(8)
+        weigh(5)
+        transpose_in(9)
+        candidates(7)
+        gates(7)
+        transpose_out((2,0))
+        finish((1,1))
+        difference(6)
+        quantise_in(9)
+        weigh(6)
+        transpose_in(10)
+        candidates(8)
+        gates(8)
+        transpose_out((2,1))
+        finish((2,0))
+        difference(7)
+        quantise_in(10)
+        weigh(7)
+        transpose_in(11)
+        candidates(9)
+        gates(9)
+        transpose_out((3,0))
+        finish((2,1))
+        difference(8)
+        quantise_in(11)
+        weigh(8)
+        transpose_in(12)
+        candidates(10)
+        gates(10)
+        transpose_out((3,1))
+        finish((3,0))
+        difference(9)
+        quantise_in(12)
+        weigh(9)
+        transpose_in(13)
+        candidates(11)
+        gates(11)
+        transpose_out((4,0))
+        finish((3,1))
+        difference(10)
+        quantise_in(13)
+        weigh(10)
+        transpose_in(14)
+        candidates(12)
+        gates(12)
+        transpose_out((4,1))
+        finish((4,0))
+        difference(11)
+        quantise_in(14)
+        weigh(11)
+        transpose_in(15)
+        candidates(13)
+        gates(13)
+        transpose_out((5,0))
+        finish((4,1))
+        difference(12)
+        quantise_in(15)
+        weigh(12)
+        transpose_in(16)
+        candidates(14)
+        gates(14)
+        transpose_out((5,1))
+        finish((5,0))
+        difference(13)
+        quantise_in(16)
+        weigh(13)
+        transpose_in(17)
+        candidates(15)
+        gates(15)
+        transpose_out((6,0))
+        finish((5,1))
+        difference(14)
+        quantise_in(17)
+        weigh(14)
+        candidates(16)
+        gates(16)
+        transpose_out((6,1))
+        finish((6,0))
+        difference(15)
+        finish((6,1))
+        weigh(15)
+        candidates(17)
+        gates(17)
+        transpose_out((7,0))
+        transpose_out((7,1))
+        difference(16)
+        finish((7,0))
+        finish((7,1))
+        weigh(16)
+        difference(17)
+        weigh(17)
+        transpose_out((8,0))
+        finish((8,0))

@@ -20,6 +20,9 @@ PASSES = 2
 HALVES = 2
 BLOCKS = [256, 512, 512, 512, 512, 512, 512, 512, 256]
 UNITS = len(BLOCKS) * HALVES
+LASTSTORE = 2
+OWN = {}
+LATE = ((7, 0), (8, 0))
 
 FLOPS = 2 * TOKENS * (PASSES * K_PASS) * (2 * D)
 
@@ -32,7 +35,7 @@ def tile_smcmr_pb_t_kernel(tc, query, weighted_ctx, W_lin, b_lin, W_gate, b_gate
         inputs = ctx.enter_context(tc.tile_pool(name="inputs", bufs=1))
         weights = ctx.enter_context(tc.tile_pool(name="weights", bufs=1))
         stage = ctx.enter_context(tc.tile_pool(name="stage", bufs=3))
-        acts = ctx.enter_context(tc.tile_pool(name="acts", bufs=2))
+        acts = ctx.enter_context(tc.tile_pool(name="acts", bufs=3))
         deltas = ctx.enter_context(tc.tile_pool(name="deltas", bufs=4))
         results = ctx.enter_context(tc.tile_pool(name="results", bufs=2))
         psum_in = ctx.enter_context(tc.psum_pool(name="psum_in", bufs=2))
@@ -92,8 +95,8 @@ def tile_smcmr_pb_t_kernel(tc, query, weighted_ctx, W_lin, b_lin, W_gate, b_gate
         scales_w = {}
         for name in ("gate", "lin"):
             grouped_w[name] = weights.tile([P, W_COLS * PACK], BF16, name="grouped_" + name, align_bytes=64)
-            codes_w[name] = weights.tile([P, W_COLS], U32, name="codes_" + name, align_bytes=64)
-            scales_w[name] = weights.tile([P, W_COLS], U8, name="scales_" + name, align_bytes=64)
+            codes_w[name] = weights.tile([P, W_COLS], U32, name="codes_" + name, align_bytes=256)
+            scales_w[name] = weights.tile([P, W_COLS], U8, name="scales_" + name, align_bytes=256)
 
         def regroup_weight(copy, name, half, passes=range(PASSES)):
             raw = raw_w[name][:].rearrange("p (g t n) -> p g t n", g=PASSES, t=PACK)
@@ -102,8 +105,8 @@ def tile_smcmr_pb_t_kernel(tc, query, weighted_ctx, W_lin, b_lin, W_gate, b_gate
             )
             for g in passes:
                 copy(
-                    out=words[:, half, g],
-                    in_=raw[:, g].rearrange("p t (j h e) -> p h e j t", h=HALVES, e=2)[:, half],
+                    out=words[:, half, g].rearrange("p e j t -> p j e t"),
+                    in_=raw[:, g].rearrange("p t (j h e) -> p h j e t", h=HALVES, e=2)[:, half],
                 )
 
         def quantise_weight(name, half):
@@ -146,8 +149,8 @@ def tile_smcmr_pb_t_kernel(tc, query, weighted_ctx, W_lin, b_lin, W_gate, b_gate
             B, g = divmod(v, PASSES)
             n = BLOCKS[B]
             if g == 0:
-                codes[B] = stage.tile([P, PASSES * n], U32, name="codes", align_bytes=64)
-                scales[B] = stage.tile([P, PASSES * n], U8, name="scales", align_bytes=64)
+                codes[B] = stage.tile([P, PASSES * n], U32, name="codes", align_bytes=256)
+                scales[B] = stage.tile([P, PASSES * n], U8, name="scales", align_bytes=256)
             nc.vector.quantize_mx(
                 out=codes[B][:, g * n : (g + 1) * n].bitcast(FP8X4),
                 scales=scales[B][:, g * n : (g + 1) * n],
@@ -198,6 +201,7 @@ def tile_smcmr_pb_t_kernel(tc, query, weighted_ctx, W_lin, b_lin, W_gate, b_gate
             q_t = grouped[B][:].rearrange("p (g c t) -> p g c t", g=PASSES, t=PACK)
             delta[s] = deltas.tile([P, 2, n], F32, name="delta")
             share = n * (5 if B < len(BLOCKS) - 1 else 0) // 8
+            share = n - OWN[n] if n in OWN else share
             for engine, tokens in ((nc.gpsimd, slice(share, n)), (nc.vector, slice(0, share))):
                 if tokens.start == tokens.stop:
                     continue
@@ -209,14 +213,23 @@ def tile_smcmr_pb_t_kernel(tc, query, weighted_ctx, W_lin, b_lin, W_gate, b_gate
                 )
 
         def weigh(s):
-            nc.vector.tensor_tensor(out=delta[s][:], in0=keep[s][:], in1=delta[s][:], op=ALU.mult)
+            n = BLOCKS[s // HALVES]
+            own = n - OWN.get(n, 0)
+            for engine, tokens in ((nc.gpsimd, slice(own, n)), (nc.vector, slice(0, own))):
+                if tokens.start < tokens.stop:
+                    engine.tensor_tensor(
+                        out=delta[s][:, :, tokens], in0=keep[s][:, :, tokens], in1=delta[s][:, :, tokens], op=ALU.mult
+                    )
 
         def transpose_out(r):
             B, b = r
             banks_out[r] = []
             for ii in range(min(BLOCKS[B] // P, 2)):
                 first = (2 * b + ii) * P
-                ot = psum_out.tile([P, PACK, P], F32, tag="ot")
+                if (B, b) in LATE:
+                    ot = psum_in.tile([P, PACK, P], F32, tag="xt")
+                else:
+                    ot = psum_out.tile([P, PACK, P], F32, tag="ot")
                 for t in range(PACK):
                     nc.tensor.transpose(
                         out=ot[:, t, :], in_=delta[2 * B + t // 2][:, t % 2, first : first + P], identity=ident[:]
@@ -235,8 +248,12 @@ def tile_smcmr_pb_t_kernel(tc, query, weighted_ctx, W_lin, b_lin, W_gate, b_gate
                 nc.vector.tensor_tensor(
                     out=o_view[:, 2 * b + ii], in0=q_view[:, 2 * b + ii], in1=turned, op=ALU.subtract
                 )
-            cols = slice(2 * b * D, (2 * b + min(tiles, 2)) * D)
-            nc.sync.dma_start(out=rows(out, B)[:, cols], in_=result[B][:, cols])
+                if B >= len(BLOCKS) - LASTSTORE:
+                    cols = slice((2 * b + ii) * D, (2 * b + ii + 1) * D)
+                    nc.sync.dma_start(out=rows(out, B)[:, cols], in_=result[B][:, cols])
+            if B < len(BLOCKS) - LASTSTORE:
+                cols = slice(2 * b * D, (2 * b + min(tiles, 2)) * D)
+                nc.sync.dma_start(out=rows(out, B)[:, cols], in_=result[B][:, cols])
 
         load_operand(0, 0)
         load_weight("lin", [0])
@@ -389,17 +406,17 @@ def tile_smcmr_pb_t_kernel(tc, query, weighted_ctx, W_lin, b_lin, W_gate, b_gate
         transpose_out((6,1))
         finish((6,0))
         difference(15)
+        difference(16)
         finish((6,1))
         weigh(15)
         candidates(17)
         gates(17)
         transpose_out((7,0))
-        transpose_out((7,1))
-        difference(16)
-        finish((7,0))
-        finish((7,1))
-        weigh(16)
         difference(17)
+        weigh(16)
+        finish((7,0))
+        transpose_out((7,1))
         weigh(17)
         transpose_out((8,0))
+        finish((7,1))
         finish((8,0))

@@ -23,6 +23,7 @@ UNITS = len(BLOCKS) * HALVES
 LASTSTORE = 2
 OWN = {}
 LATE = ((7, 0), (8, 0))
+SPLIT = '--SV'
 
 FLOPS = 2 * TOKENS * (PASSES * K_PASS) * (2 * D)
 
@@ -35,6 +36,7 @@ def tile_smcmr_pb_t_kernel(tc, query, weighted_ctx, W_lin, b_lin, W_gate, b_gate
         inputs = ctx.enter_context(tc.tile_pool(name="inputs", bufs=1))
         weights = ctx.enter_context(tc.tile_pool(name="weights", bufs=1))
         stage = ctx.enter_context(tc.tile_pool(name="stage", bufs=3))
+        apart_pool = ctx.enter_context(tc.tile_pool(name="apart_pool", bufs=6))
         acts = ctx.enter_context(tc.tile_pool(name="acts", bufs=3))
         deltas = ctx.enter_context(tc.tile_pool(name="deltas", bufs=4))
         results = ctx.enter_context(tc.tile_pool(name="results", bufs=2))
@@ -126,6 +128,24 @@ def tile_smcmr_pb_t_kernel(tc, query, weighted_ctx, W_lin, b_lin, W_gate, b_gate
         banks_out = {}
         result = {}
 
+        halves_apart = {}
+
+        def split_words(v, names):
+            B, g = divmod(v, PASSES)
+            words = (q_sb[B] if g == 0 else c_sb[B])[:].bitcast(F32)
+            tiles = BLOCKS[B] // P
+            for name, copy in (("V", nc.vector.tensor_copy), ("S", nc.scalar.copy), ("G", nc.gpsimd.tensor_copy)):
+                mine = [i for i in range(tiles) if SPLIT[i] == name]
+                if name in names and mine:
+                    i0, count = mine[0], len(mine)
+                    apart = apart_pool.tile([P, count * 2 * P], F32, name="apart" + name)
+                    for i in mine:
+                        halves_apart[v, i] = apart[:, (i - i0) * 2 * P : (i - i0 + 1) * 2 * P]
+                    copy(
+                        out=apart[:].rearrange("p (i u w) -> p i u w", u=2, w=P),
+                        in_=words[:, i0 * 2 * P : (i0 + count) * 2 * P].rearrange("p (i w u) -> p i u w", u=2, w=P),
+                    )
+
         def transpose_in(v):
             B, g = divmod(v, PASSES)
             n = BLOCKS[B]
@@ -138,8 +158,11 @@ def tile_smcmr_pb_t_kernel(tc, query, weighted_ctx, W_lin, b_lin, W_gate, b_gate
                 xt = psum_in.tile([P, 2, width], F32, tag="xt")
                 for u in range(2):
                     for ii in range(width // P):
-                        first = (2 * b + ii) * 2 * P
-                        in_words = words[:, first + u : first + 2 * P : 2]
+                        if (v, 2 * b + ii) in halves_apart:
+                            in_words = halves_apart[v, 2 * b + ii][:, u * P : (u + 1) * P]
+                        else:
+                            first = (2 * b + ii) * 2 * P
+                            in_words = words[:, first + u : first + 2 * P : 2]
                         nc.tensor.transpose(out=xt[:, u, ii * P : (ii + 1) * P], in_=in_words, identity=ident[:])
                 nc.scalar.copy(
                     out=pairs[:, g, b * width : (b + 1) * width, :], in_=xt[:].rearrange("p u c -> p c u")
@@ -298,6 +321,7 @@ def tile_smcmr_pb_t_kernel(tc, query, weighted_ctx, W_lin, b_lin, W_gate, b_gate
         candidates(2)
         gates(2)
         difference(1)
+        split_words(6, "VSG")
         quantise_in(4)
         weigh(1)
         transpose_in(5)
@@ -305,6 +329,7 @@ def tile_smcmr_pb_t_kernel(tc, query, weighted_ctx, W_lin, b_lin, W_gate, b_gate
         gates(3)
         transpose_out((0,0))
         difference(2)
+        split_words(7, "VSG")
         quantise_in(5)
         weigh(2)
         transpose_in(6)
@@ -312,6 +337,7 @@ def tile_smcmr_pb_t_kernel(tc, query, weighted_ctx, W_lin, b_lin, W_gate, b_gate
         gates(4)
         finish((0,0))
         difference(3)
+        split_words(8, "VSG")
         quantise_in(6)
         weigh(3)
         transpose_in(7)
@@ -319,6 +345,7 @@ def tile_smcmr_pb_t_kernel(tc, query, weighted_ctx, W_lin, b_lin, W_gate, b_gate
         gates(5)
         transpose_out((1,0))
         difference(4)
+        split_words(9, "VSG")
         quantise_in(7)
         weigh(4)
         transpose_in(8)
@@ -327,6 +354,7 @@ def tile_smcmr_pb_t_kernel(tc, query, weighted_ctx, W_lin, b_lin, W_gate, b_gate
         transpose_out((1,1))
         finish((1,0))
         difference(5)
+        split_words(10, "VSG")
         quantise_in(8)
         weigh(5)
         transpose_in(9)
@@ -335,6 +363,7 @@ def tile_smcmr_pb_t_kernel(tc, query, weighted_ctx, W_lin, b_lin, W_gate, b_gate
         transpose_out((2,0))
         finish((1,1))
         difference(6)
+        split_words(11, "VSG")
         quantise_in(9)
         weigh(6)
         transpose_in(10)
@@ -343,6 +372,7 @@ def tile_smcmr_pb_t_kernel(tc, query, weighted_ctx, W_lin, b_lin, W_gate, b_gate
         transpose_out((2,1))
         finish((2,0))
         difference(7)
+        split_words(12, "VSG")
         quantise_in(10)
         weigh(7)
         transpose_in(11)
@@ -351,6 +381,7 @@ def tile_smcmr_pb_t_kernel(tc, query, weighted_ctx, W_lin, b_lin, W_gate, b_gate
         transpose_out((3,0))
         finish((2,1))
         difference(8)
+        split_words(13, "VSG")
         quantise_in(11)
         weigh(8)
         transpose_in(12)
@@ -359,6 +390,7 @@ def tile_smcmr_pb_t_kernel(tc, query, weighted_ctx, W_lin, b_lin, W_gate, b_gate
         transpose_out((3,1))
         finish((3,0))
         difference(9)
+        split_words(14, "VSG")
         quantise_in(12)
         weigh(9)
         transpose_in(13)
@@ -367,6 +399,7 @@ def tile_smcmr_pb_t_kernel(tc, query, weighted_ctx, W_lin, b_lin, W_gate, b_gate
         transpose_out((4,0))
         finish((3,1))
         difference(10)
+        split_words(15, "VSG")
         quantise_in(13)
         weigh(10)
         transpose_in(14)
@@ -375,6 +408,7 @@ def tile_smcmr_pb_t_kernel(tc, query, weighted_ctx, W_lin, b_lin, W_gate, b_gate
         transpose_out((4,1))
         finish((4,0))
         difference(11)
+        split_words(16, "VSG")
         quantise_in(14)
         weigh(11)
         transpose_in(15)
@@ -383,6 +417,7 @@ def tile_smcmr_pb_t_kernel(tc, query, weighted_ctx, W_lin, b_lin, W_gate, b_gate
         transpose_out((5,0))
         finish((4,1))
         difference(12)
+        split_words(17, "VSG")
         quantise_in(15)
         weigh(12)
         transpose_in(16)

@@ -20,10 +20,13 @@ PASSES = 2
 HALVES = 2
 BLOCKS = [256, 512, 512, 512, 512, 512, 512, 512, 256]
 UNITS = len(BLOCKS) * HALVES
+SHARES = {16: 0, 17: 8}
+OVER = 0
 LASTSTORE = 2
 OWN = {}
 LATE = ((7, 0), (8, 0))
 SPLIT = '--SV'
+SPLITS = {4: '--VV', 5: '--VV'}
 
 FLOPS = 2 * TOKENS * (PASSES * K_PASS) * (2 * D)
 
@@ -119,6 +122,23 @@ def tile_smcmr_pb_t_kernel(tc, query, weighted_ctx, W_lin, b_lin, W_gate, b_gate
                 in_=grouped_w[name][:, half * PASSES * 2 * P * PACK : (half + 1) * PASSES * 2 * P * PACK],
             )
 
+        def quantise_weight_pass(name, half, g):
+            first = (half * PASSES + g) * 2 * P
+            cols = slice(first, first + 2 * P)
+            nc.vector.quantize_mx(
+                out=codes_w[name][:, cols].bitcast(FP8X4),
+                scales=scales_w[name][:, cols],
+                in_=grouped_w[name][:, first * PACK : (first + 2 * P) * PACK],
+            )
+
+        def regroup_part(copy, name, half, g, first, last):
+            raw = raw_w[name][:].rearrange("p (g t n) -> p g t n", g=PASSES, t=PACK)
+            words = grouped_w[name][:].rearrange("p (u g e j t) -> p u g e j t", u=HALVES, g=PASSES, e=2, t=PACK)
+            copy(
+                out=words[:, half, g].rearrange("p e j t -> p j e t")[:, first:last],
+                in_=raw[:, g].rearrange("p t (j h e) -> p h j e t", h=HALVES, e=2)[:, half, first:last],
+            )
+
         grouped = {}
         codes = {}
         scales = {}
@@ -135,7 +155,7 @@ def tile_smcmr_pb_t_kernel(tc, query, weighted_ctx, W_lin, b_lin, W_gate, b_gate
             words = (q_sb[B] if g == 0 else c_sb[B])[:].bitcast(F32)
             tiles = BLOCKS[B] // P
             for name, copy in (("V", nc.vector.tensor_copy), ("S", nc.scalar.copy), ("G", nc.gpsimd.tensor_copy)):
-                mine = [i for i in range(tiles) if SPLIT[i] == name]
+                mine = [i for i in range(tiles) if SPLITS.get(v, SPLIT)[i] == name]
                 if name in names and mine:
                     i0, count = mine[0], len(mine)
                     apart = apart_pool.tile([P, count * 2 * P], F32, name="apart" + name)
@@ -225,7 +245,8 @@ def tile_smcmr_pb_t_kernel(tc, query, weighted_ctx, W_lin, b_lin, W_gate, b_gate
             delta[s] = deltas.tile([P, 2, n], F32, name="delta")
             share = n * (5 if B < len(BLOCKS) - 1 else 0) // 8
             share = n - OWN[n] if n in OWN else share
-            for engine, tokens in ((nc.gpsimd, slice(share, n)), (nc.vector, slice(0, share))):
+            share = n * SHARES[s] // 8 if s in SHARES else share
+            for engine, tokens in ((nc.vector, slice(0, share)), (nc.gpsimd, slice(share - OVER if share else 0, n)))[:: 1 if OVER else -1]:
                 if tokens.start == tokens.stop:
                     continue
                 engine.tensor_tensor(
@@ -243,6 +264,9 @@ def tile_smcmr_pb_t_kernel(tc, query, weighted_ctx, W_lin, b_lin, W_gate, b_gate
                     engine.tensor_tensor(
                         out=delta[s][:, :, tokens], in0=keep[s][:, :, tokens], in1=delta[s][:, :, tokens], op=ALU.mult
                     )
+
+        def weigh_elsewhere(s):
+            nc.gpsimd.tensor_tensor(out=delta[s][:], in0=keep[s][:], in1=delta[s][:], op=ALU.mult)
 
         def transpose_out(r):
             B, b = r
@@ -282,27 +306,28 @@ def tile_smcmr_pb_t_kernel(tc, query, weighted_ctx, W_lin, b_lin, W_gate, b_gate
         load_weight("lin", [0])
         load_operand(0, 1)
         load_weight("lin", [1])
-        load_biases()
         load_weight("gate", [0])
         load_weight("gate", [1])
+        load_biases()
         load_operand(1, 0)
         load_operand(1, 1)
         for B in range(2, len(BLOCKS)):
             load_block(B)
         V, S = nc.vector.tensor_copy, nc.scalar.copy
         transpose_in(0)
-        regroup_weight(V, "lin", 0, [0])
-        regroup_weight(V, "lin", 1, [0])
-        quantise_in(0)
-        regroup_weight(V, "lin", 0, [1])
-        regroup_weight(S, "lin", 1, [1])
         transpose_in(1)
-        spread_biases()
-        quantise_weight("lin", 0)
+        regroup_weight(V, "lin", 0, [0])
+        quantise_in(0)
+        regroup_weight(V, "lin", 1, [0])
+        quantise_weight_pass("lin", 0, 0)
+        regroup_weight(V, "lin", 0, [1])
         quantise_in(1)
+        quantise_weight_pass("lin", 0, 1)
+        spread_biases()
+        regroup_weight(S, "lin", 1, [1])
         quantise_weight("lin", 1)
-        regroup_weight(S, "gate", 1, [0])
         candidates(0)
+        regroup_weight(S, "gate", 1, [0])
         candidates(1)
         regroup_weight(V, "gate", 0, [0])
         regroup_weight(V, "gate", 0, [1])
@@ -310,9 +335,11 @@ def tile_smcmr_pb_t_kernel(tc, query, weighted_ctx, W_lin, b_lin, W_gate, b_gate
         transpose_in(2)
         regroup_weight(V, "gate", 1, [1])
         quantise_weight("gate", 1)
+        split_words(4, "VSG")
         gates(0)
         transpose_in(3)
         quantise_in(2)
+        split_words(5, "VSG")
         gates(1)
         difference(0)
         quantise_in(3)

@@ -59,7 +59,6 @@ def tile_smcmr_pb_t_kernel(tc, query, weighted_ctx, W_lin, b_lin, W_gate, b_gate
         zero = const.tile([P, 1], F32)
         nc.vector.memset(zero[:], 0.0)
         warm = const.tile([P, 1], F32)
-        nc.scalar.activation(out=warm[:], in_=zero[:], func=ACT.Sigmoid)
 
         q_sb = {}
         c_sb = {}
@@ -86,9 +85,9 @@ def tile_smcmr_pb_t_kernel(tc, query, weighted_ctx, W_lin, b_lin, W_gate, b_gate
         bias_lin = const.tile([P, PACK], F32)
         bias_gate_neg = const.tile([P, PACK], F32)
 
-        def load_biases():
-            nc.sync.dma_start(out=bias_raw[:, 0:PACK], in_=b_lin.rearrange("(p t) -> p t", t=PACK))
-            nc.sync.dma_start(out=bias_raw[:, 64 : 64 + PACK], in_=b_gate.rearrange("(p t) -> p t", t=PACK))
+        def load_biases(queue=nc.sync):
+            queue.dma_start(out=bias_raw[:, 0:PACK], in_=b_lin.rearrange("(p t) -> p t", t=PACK))
+            queue.dma_start(out=bias_raw[:, 64 : 64 + PACK], in_=b_gate.rearrange("(p t) -> p t", t=PACK))
 
         def spread_biases():
             nc.vector.tensor_copy(out=bias_lin[:], in_=bias_raw[:, 0:PACK])
@@ -302,13 +301,14 @@ def tile_smcmr_pb_t_kernel(tc, query, weighted_ctx, W_lin, b_lin, W_gate, b_gate
                 cols = slice(2 * b * D, (2 * b + min(tiles, 2)) * D)
                 nc.sync.dma_start(out=rows(out, B)[:, cols], in_=result[B][:, cols])
 
+        load_biases(nc.scalar)
+        nc.scalar.activation(out=warm[:], in_=zero[:], func=ACT.Sigmoid)
         load_operand(0, 0)
         load_weight("lin", [0])
         load_operand(0, 1)
         load_weight("lin", [1])
         load_weight("gate", [0])
         load_weight("gate", [1])
-        load_biases()
         load_operand(1, 0)
         load_operand(1, 1)
         for B in range(2, len(BLOCKS)):
@@ -316,6 +316,7 @@ def tile_smcmr_pb_t_kernel(tc, query, weighted_ctx, W_lin, b_lin, W_gate, b_gate
         V, S = nc.vector.tensor_copy, nc.scalar.copy
         transpose_in(0)
         transpose_in(1)
+        spread_biases()
         regroup_weight(V, "lin", 0, [0])
         quantise_in(0)
         regroup_weight(V, "lin", 1, [0])
@@ -323,7 +324,6 @@ def tile_smcmr_pb_t_kernel(tc, query, weighted_ctx, W_lin, b_lin, W_gate, b_gate
         regroup_weight(V, "lin", 0, [1])
         quantise_in(1)
         quantise_weight_pass("lin", 0, 1)
-        spread_biases()
         regroup_weight(S, "lin", 1, [1])
         quantise_weight("lin", 1)
         candidates(0)

from contextlib import ExitStack

import concourse.mybir as mybir
from concourse.masks import make_identity

F32 = mybir.dt.float32
BF16 = mybir.dt.bfloat16
U32 = mybir.dt.uint32
U8 = mybir.dt.uint8
FP8X4 = mybir.dt.float8_e4m3fn_x4
ACT = mybir.ActivationFunctionType
ALU = mybir.AluOpType

P = 128
PACK = 4
K_PASS = P * PACK
TOKENS = 4096
D = 512
PASSES = 2
HALVES = 2
BLOCKS = [256, 512, 512, 512, 512, 512, 512, 512, 256]
UNITS = len(BLOCKS) * HALVES
SHARES = {16: 0, 17: 8}
OVER = 0
LASTSTORE = 2
OWN = {}
LATE = ((7, 0), (8, 0))
SPLIT = '--SV'
SPLITS = {4: '--VV', 5: '--VV'}

FLOPS = 2 * TOKENS * (PASSES * K_PASS) * (2 * D)


def tile_smcmr_pb_t_kernel(tc, query, weighted_ctx, W_lin, b_lin, W_gate, b_gate, out):
    nc = tc.nc
    with ExitStack() as ctx:
        ctx.enter_context(tc.manual_schedule())
        const = ctx.enter_context(tc.tile_pool(name="const", bufs=1))
        inputs = ctx.enter_context(tc.tile_pool(name="inputs", bufs=1))
        weights = ctx.enter_context(tc.tile_pool(name="weights", bufs=1))
        stage = ctx.enter_context(tc.tile_pool(name="stage", bufs=3))
        apart_pool = ctx.enter_context(tc.tile_pool(name="apart_pool", bufs=6))
        acts = ctx.enter_context(tc.tile_pool(name="acts", bufs=3))
        deltas = ctx.enter_context(tc.tile_pool(name="deltas", bufs=4))
        results = ctx.enter_context(tc.tile_pool(name="results", bufs=2))
        psum_in = ctx.enter_context(tc.psum_pool(name="psum_in", bufs=2))
        psum_acc = ctx.enter_context(tc.psum_pool(name="psum_acc", bufs=4))
        psum_out = ctx.enter_context(tc.psum_pool(name="psum_out", bufs=2))

        starts = [sum(BLOCKS[:B]) for B in range(len(BLOCKS))]

        def rows(array, B):
            block = array.flatten_outer_dims()[starts[B] : starts[B] + BLOCKS[B], :]
            return block.rearrange("(p i) f -> p (i f)", p=P)

        ident = const.tile([P, P], F32)
        make_identity(nc, ident[:])
        bias_raw = const.tile([P, 2 * 64], BF16)
        zero = const.tile([P, 1], F32)
        nc.vector.memset(zero[:], 0.0)
        warm = const.tile([P, 1], F32)

        q_sb = {}
        c_sb = {}

        def load_operand(B, g):
            kept, array, name = ((q_sb, query, "q"), (c_sb, weighted_ctx, "c"))[g]
            kept[B] = inputs.tile([P, BLOCKS[B] // P * D], BF16, name="%s%d" % (name, B))
            nc.sync.dma_start(out=kept[B][:], in_=rows(array, B))

        def load_block(B):
            for g in range(PASSES):
                load_operand(B, g)

        raw_w = {}

        def load_weight(name, passes=range(PASSES)):
            W = {"lin": W_lin, "gate": W_gate}[name]
            if name not in raw_w:
                raw_w[name] = weights.tile([P, PASSES * PACK * D], BF16, name="raw_" + name)
            rows_w = W.rearrange("(g p t) n -> g p (t n)", g=PASSES, t=PACK)
            for g in passes:
                nc.sync.dma_start(out=raw_w[name][:, g * PACK * D : (g + 1) * PACK * D], in_=rows_w[g])

        bias_lin = const.tile([P, PACK], F32)
        bias_gate_neg = const.tile([P, PACK], F32)

        def load_biases(queue=nc.sync):
            queue.dma_start(out=bias_raw[:, 0:PACK], in_=b_lin.rearrange("(p t) -> p t", t=PACK))
            queue.dma_start(out=bias_raw[:, 64 : 64 + PACK], in_=b_gate.rearrange("(p t) -> p t", t=PACK))

        def spread_biases():
            nc.vector.tensor_copy(out=bias_lin[:], in_=bias_raw[:, 0:PACK])
            nc.vector.tensor_scalar_mul(out=bias_gate_neg[:], in0=bias_raw[:, 64 : 64 + PACK], scalar1=-1.0)

        W_COLS = HALVES * PASSES * 2 * P
        grouped_w = {}
        codes_w = {}
        scales_w = {}
        for name in ("gate", "lin"):
            grouped_w[name] = weights.tile([P, W_COLS * PACK], BF16, name="grouped_" + name, align_bytes=64)
            codes_w[name] = weights.tile([P, W_COLS], U32, name="codes_" + name, align_bytes=256)
            scales_w[name] = weights.tile([P, W_COLS], U8, name="scales_" + name, align_bytes=256)

        def regroup_weight(copy, name, half, passes=range(PASSES)):
            raw = raw_w[name][:].rearrange("p (g t n) -> p g t n", g=PASSES, t=PACK)
            words = grouped_w[name][:].rearrange(
                "p (u g e j t) -> p u g e j t", u=HALVES, g=PASSES, e=2, t=PACK
            )
            for g in passes:
                copy(
                    out=words[:, half, g].rearrange("p e j t -> p j e t"),
                    in_=raw[:, g].rearrange("p t (j h e) -> p h j e t", h=HALVES, e=2)[:, half],
                )

        def quantise_weight(name, half):
            cols = slice(half * PASSES * 2 * P, (half + 1) * PASSES * 2 * P)
            nc.vector.quantize_mx(
                out=codes_w[name][:, cols].bitcast(FP8X4),
                scales=scales_w[name][:, cols],
                in_=grouped_w[name][:, half * PASSES * 2 * P * PACK : (half + 1) * PASSES * 2 * P * PACK],
            )

        def quantise_weight_pass(name, half, g):
            first = (half * PASSES + g) * 2 * P
            cols = slice(first, first + 2 * P)
            nc.vector.quantize_mx(
                out=codes_w[name][:, cols].bitcast(FP8X4),
                scales=scales_w[name][:, cols],
                in_=grouped_w[name][:, first * PACK : (first + 2 * P) * PACK],
            )

        def regroup_part(copy, name, half, g, first, last):
            raw = raw_w[name][:].rearrange("p (g t n) -> p g t n", g=PASSES, t=PACK)
            words = grouped_w[name][:].rearrange("p (u g e j t) -> p u g e j t", u=HALVES, g=PASSES, e=2, t=PACK)
            copy(
                out=words[:, half, g].rearrange("p e j t -> p j e t")[:, first:last],
                in_=raw[:, g].rearrange("p t (j h e) -> p h j e t", h=HALVES, e=2)[:, half, first:last],
            )

        grouped = {}
        codes = {}
        scales = {}
        keep = {}
        cand = {}
        delta = {}
        banks_out = {}
        result = {}

        halves_apart = {}

        def split_words(v, names):
            B, g = divmod(v, PASSES)
            words = (q_sb[B] if g == 0 else c_sb[B])[:].bitcast(F32)
            tiles = BLOCKS[B] // P
            for name, copy in (("V", nc.vector.tensor_copy), ("S", nc.scalar.copy), ("G", nc.gpsimd.tensor_copy)):
                mine = [i for i in range(tiles) if SPLITS.get(v, SPLIT)[i] == name]
                if name in names and mine:
                    i0, count = mine[0], len(mine)
                    apart = apart_pool.tile([P, count * 2 * P], F32, name="apart" + name)
                    for i in mine:
                        halves_apart[v, i] = apart[:, (i - i0) * 2 * P : (i - i0 + 1) * 2 * P]
                    copy(
                        out=apart[:].rearrange("p (i u w) -> p i u w", u=2, w=P),
                        in_=words[:, i0 * 2 * P : (i0 + count) * 2 * P].rearrange("p (i w u) -> p i u w", u=2, w=P),
                    )

        def transpose_in(v):
            B, g = divmod(v, PASSES)
            n = BLOCKS[B]
            if g == 0:
                grouped[B] = stage.tile([P, PASSES * n * PACK], BF16, name="grouped", align_bytes=64)
            words = (q_sb[B] if g == 0 else c_sb[B])[:].bitcast(F32)
            pairs = grouped[B][:].bitcast(F32).rearrange("p (g c u) -> p g c u", g=PASSES, u=2)
            width = min(n, 2 * P)
            for b in range(n // width):
                xt = psum_in.tile([P, 2, width], F32, tag="xt")
                for u in range(2):
                    for ii in range(width // P):
                        if (v, 2 * b + ii) in halves_apart:
                            in_words = halves_apart[v, 2 * b + ii][:, u * P : (u + 1) * P]
                        else:
                            first = (2 * b + ii) * 2 * P
                            in_words = words[:, first + u : first + 2 * P : 2]
                        nc.tensor.transpose(out=xt[:, u, ii * P : (ii + 1) * P], in_=in_words, identity=ident[:])
                nc.scalar.copy(
                    out=pairs[:, g, b * width : (b + 1) * width, :], in_=xt[:].rearrange("p u c -> p c u")
                )

        def quantise_in(v):
            B, g = divmod(v, PASSES)
            n = BLOCKS[B]
            if g == 0:
                codes[B] = stage.tile([P, PASSES * n], U32, name="codes", align_bytes=256)
                scales[B] = stage.tile([P, PASSES * n], U8, name="scales", align_bytes=256)
            nc.vector.quantize_mx(
                out=codes[B][:, g * n : (g + 1) * n].bitcast(FP8X4),
                scales=scales[B][:, g * n : (g + 1) * n],
                in_=grouped[B][:, g * n * PACK : (g + 1) * n * PACK],
            )

        def product(name, B, half, e):
            n = BLOCKS[B]
            acc = psum_acc.tile([P, n], F32, tag="acc")
            for g in range(PASSES):
                first = ((half * PASSES + g) * 2 + e) * P
                nc.tensor.matmul_mx(
                    out=acc[:],
                    lhsT=codes_w[name][:, first : first + P].bitcast(FP8X4),
                    lhsT_scale=scales_w[name][:, first : first + P],
                    rhs=codes[B][:, g * n : (g + 1) * n].bitcast(FP8X4),
                    rhs_scale=scales[B][:, g * n : (g + 1) * n],
                    start=(g == 0),
                    stop=(g == PASSES - 1),
                )
            return acc

        def candidates(s):
            B, half = divmod(s, HALVES)
            n = BLOCKS[B]
            cand[s] = acts.tile([P, 2, n], F32, name="cand")
            for e in range(2):
                t = 2 * half + e
                acc = product("lin", B, half, e)
                nc.scalar.activation(
                    out=cand[s][:, e, :], in_=acc[:], func=ACT.Tanh, bias=bias_lin[:, t : t + 1], scale=1.0
                )

        def gates(s):
            B, half = divmod(s, HALVES)
            n = BLOCKS[B]
            keep[s] = acts.tile([P, 2, n], F32, name="keep")
            for e in range(2):
                t = 2 * half + e
                acc = product("gate", B, half, e)
                nc.scalar.activation(
                    out=keep[s][:, e, :], in_=acc[:], func=ACT.Sigmoid, bias=bias_gate_neg[:, t : t + 1], scale=-1.0
                )

        def difference(s):
            B, half = divmod(s, HALVES)
            n = BLOCKS[B]
            q_t = grouped[B][:].rearrange("p (g c t) -> p g c t", g=PASSES, t=PACK)
            delta[s] = deltas.tile([P, 2, n], F32, name="delta")
            share = n * (5 if B < len(BLOCKS) - 1 else 0) // 8
            share = n - OWN[n] if n in OWN else share
            share = n * SHARES[s] // 8 if s in SHARES else share
            for engine, tokens in ((nc.vector, slice(0, share)), (nc.gpsimd, slice(share - OVER if share else 0, n)))[:: 1 if OVER else -1]:
                if tokens.start == tokens.stop:
                    continue
                engine.tensor_tensor(
                    out=delta[s][:, :, tokens],
                    in0=q_t[:, 0, tokens, 2 * half : 2 * half + 2].rearrange("p c e -> p e c"),
                    in1=cand[s][:, :, tokens],
                    op=ALU.subtract,
                )

        def weigh(s):
            n = BLOCKS[s // HALVES]
            own = n - OWN.get(n, 0)
            for engine, tokens in ((nc.gpsimd, slice(own, n)), (nc.vector, slice(0, own))):
                if tokens.start < tokens.stop:
                    engine.tensor_tensor(
                        out=delta[s][:, :, tokens], in0=keep[s][:, :, tokens], in1=delta[s][:, :, tokens], op=ALU.mult
                    )

        def weigh_elsewhere(s):
            nc.gpsimd.tensor_tensor(out=delta[s][:], in0=keep[s][:], in1=delta[s][:], op=ALU.mult)

        def transpose_out(r):
            B, b = r
            banks_out[r] = []
            for ii in range(min(BLOCKS[B] // P, 2)):
                first = (2 * b + ii) * P
                if (B, b) in LATE:
                    ot = psum_in.tile([P, PACK, P], F32, tag="xt")
                else:
                    ot = psum_out.tile([P, PACK, P], F32, tag="ot")
                for t in range(PACK):
                    nc.tensor.transpose(
                        out=ot[:, t, :], in_=delta[2 * B + t // 2][:, t % 2, first : first + P], identity=ident[:]
                    )
                banks_out[r].append(ot)

        def finish(r):
            B, b = r
            tiles = BLOCKS[B] // P
            if b == 0:
                result[B] = results.tile([P, tiles * D], F32, name="result")
            o_view = result[B][:].rearrange("p (i j t) -> p i j t", i=tiles, t=PACK)
            q_view = q_sb[B][:].rearrange("p (i j t) -> p i j t", i=tiles, t=PACK)
            for ii in range(min(tiles, 2)):
                turned = banks_out[r][ii][:].rearrange("p t j -> p j t")
                nc.vector.tensor_tensor(
                    out=o_view[:, 2 * b + ii], in0=q_view[:, 2 * b + ii], in1=turned, op=ALU.subtract
                )
                if B >= len(BLOCKS) - LASTSTORE:
                    cols = slice((2 * b + ii) * D, (2 * b + ii + 1) * D)
                    nc.sync.dma_start(out=rows(out, B)[:, cols], in_=result[B][:, cols])
            if B < len(BLOCKS) - LASTSTORE:
                cols = slice(2 * b * D, (2 * b + min(tiles, 2)) * D)
                nc.sync.dma_start(out=rows(out, B)[:, cols], in_=result[B][:, cols])

        load_biases(nc.scalar)
        nc.scalar.activation(out=warm[:], in_=zero[:], func=ACT.Sigmoid)
        load_operand(0, 0)
        load_weight("lin", [0])
        load_operand(0, 1)
        load_weight("lin", [1])
        load_weight("gate", [0])
        load_weight("gate", [1])
        load_operand(1, 0)
        load_operand(1, 1)
        for B in range(2, len(BLOCKS)):
            load_block(B)
        V, S = nc.vector.tensor_copy, nc.scalar.copy
        transpose_in(0)
        transpose_in(1)
        spread_biases()
        regroup_weight(V, "lin", 0, [0])
        quantise_in(0)
        regroup_weight(V, "lin", 1, [0])
        quantise_weight_pass("lin", 0, 0)
        regroup_weight(V, "lin", 0, [1])
        quantise_in(1)
        quantise_weight_pass("lin", 0, 1)
        regroup_weight(S, "lin", 1, [1])
        quantise_weight("lin", 1)
        candidates(0)
        regroup_weight(S, "gate", 1, [0])
        candidates(1)
        regroup_weight(V, "gate", 0, [0])
        regroup_weight(V, "gate", 0, [1])
        quantise_weight("gate", 0)
        transpose_in(2)
        regroup_weight(V, "gate", 1, [1])
        quantise_weight("gate", 1)
        split_words(4, "VSG")
        gates(0)
        transpose_in(3)
        quantise_in(2)
        split_words(5, "VSG")
        gates(1)
        difference(0)
        quantise_in(3)
        weigh(0)
        transpose_in(4)
        candidates(2)
        gates(2)
        difference(1)
        split_words(6, "VSG")
        quantise_in(4)
        weigh(1)
        transpose_in(5)
        candidates(3)
        gates(3)
        transpose_out((0,0))
        difference(2)
        split_words(7, "VSG")
        quantise_in(5)
        weigh(2)
        transpose_in(6)
        candidates(4)
        gates(4)
        finish((0,0))
        difference(3)
        split_words(8, "VSG")
        quantise_in(6)
        weigh(3)
        transpose_in(7)
        candidates(5)
        gates(5)
        transpose_out((1,0))
        difference(4)
        split_words(9, "VSG")
        quantise_in(7)
        weigh(4)
        transpose_in(8)
        candidates(6)
        gates(6)
        transpose_out((1,1))
        finish((1,0))
        difference(5)
        split_words(10, "VSG")
        quantise_in(8)
        weigh(5)
        transpose_in(9)
        candidates(7)
        gates(7)
        transpose_out((2,0))
        finish((1,1))
        difference(6)
        split_words(11, "VSG")
        quantise_in(9)
        weigh(6)
        transpose_in(10)
        candidates(8)
        gates(8)
        transpose_out((2,1))
        finish((2,0))
        difference(7)
        split_words(12, "VSG")
        quantise_in(10)
        weigh(7)
        transpose_in(11)
        candidates(9)
        gates(9)
        transpose_out((3,0))
        finish((2,1))
        difference(8)
        split_words(13, "VSG")
        quantise_in(11)
        weigh(8)
        transpose_in(12)
        candidates(10)
        gates(10)
        transpose_out((3,1))
        finish((3,0))
        difference(9)
        split_words(14, "VSG")
        quantise_in(12)
        weigh(9)
        transpose_in(13)
        candidates(11)
        gates(11)
        transpose_out((4,0))
        finish((3,1))
        difference(10)
        split_words(15, "VSG")
        quantise_in(13)
        weigh(10)
        transpose_in(14)
        candidates(12)
        gates(12)
        transpose_out((4,1))
        finish((4,0))
        difference(11)
        split_words(16, "VSG")
        quantise_in(14)
        weigh(11)
        transpose_in(15)
        candidates(13)
        gates(13)
        transpose_out((5,0))
        finish((4,1))
        difference(12)
        split_words(17, "VSG")
        quantise_in(15)
        weigh(12)
        transpose_in(16)
        candidates(14)
        gates(14)
        transpose_out((5,1))
        finish((5,0))
        difference(13)
        quantise_in(16)
        weigh(13)
        transpose_in(17)
        candidates(15)
        gates(15)
        transpose_out((6,0))
        finish((5,1))
        difference(14)
        quantise_in(17)
        weigh(14)
        candidates(16)
        gates(16)
        transpose_out((6,1))
        finish((6,0))
        difference(15)
        difference(16)
        finish((6,1))
        weigh(15)
        candidates(17)
        gates(17)
        transpose_out((7,0))
        difference(17)
        weigh(16)
        finish((7,0))
        transpose_out((7,1))
        weigh(17)
        transpose_out((8,0))
        finish((7,1))
        finish((8,0))
